import numpy as np
import ml_dtypes

BF16 = ml_dtypes.bfloat16


def bf(x):
    return np.asarray(x, np.float32).astype(BF16)


def f32(x):
    return np.asarray(x, np.float32)


def f64(x):
    return np.asarray(x).astype(np.float64)


def striped(idx):
    return np.tile(idx.reshape(-1, 16).T, (8, 1))


V, D, E, M, N = 2048, 128, 256, 512, 1024


def setup_inputs():
    return {"table": bf(np.random.standard_normal((D, V))), "skill": bf(np.random.standard_normal((D, N))), "w_item": bf(np.random.standard_normal((D, M)) / np.sqrt(E)), "w_skill": bf(np.random.standard_normal((D, M)) / np.sqrt(E)), "b": f32(0.1 * np.random.standard_normal((E, 1))), "lab": f32(np.random.random((1, N)) < 0.5), "offs": striped(np.random.permutation(np.tile(np.arange(V), 2))[:N])}


def reference(table, skill, w_item, w_skill, b, lab, offs):
    idx = offs[:16].T.reshape(-1)
    u = f64(w_item).T @ f64(table)[:, idx] + f64(w_skill).T @ f64(skill)
    l = f64(lab)
    return np.maximum(l * u[:E] + (1.0 - l) * u[E:] + f64(b), 0.0)

@@ -1,0 +1,88 @@
+import concourse.mybir as mybir
+
+BF16, F32, U16 = mybir.dt.bfloat16, mybir.dt.float32, mybir.dt.uint16
+MULT, ADD = mybir.AluOpType.mult, mybir.AluOpType.add
+RELU = mybir.ActivationFunctionType.Relu
+
+P = 128
+ITEMS = 2048
+N = 1024
+E = 256
+PIECE = 512
+PER_COLUMN = 16
+
+FLOPS = 2 * (2 * E) * N * (2 * P)
+
+
+def tile_tsakt_kernel(tc, table, skill, w_item, w_skill, b, lab, offs, out):
+    nc = tc.nc
+    with (
+        tc.tile_pool(name="held", bufs=1) as held,
+        tc.tile_pool(name="work", bufs=4) as work,
+        tc.psum_pool(name="psum", bufs=4) as psum,
+    ):
+        offsets = held.tile([P, N // PER_COLUMN], U16, name="offsets")
+        nc.sync.dma_start(offsets[:], offs)
+        w_skill_sb = held.tile([P, 2 * E], BF16, name="w_skill_sb")
+        nc.scalar.dma_start(w_skill_sb[:], w_skill)
+        skill_sb = held.tile([P, N], BF16, name="skill_sb")
+        nc.scalar.dma_start(skill_sb[:], skill)
+        table_sb = held.tile([P, ITEMS], BF16, name="table_sb")
+        nc.sync.dma_start(table_sb[:], table)
+        w_item_sb = held.tile([P, 2 * E], BF16, name="w_item_sb")
+        nc.scalar.dma_start(w_item_sb[:], w_item)
+
+        is_right = held.tile([P, N], F32, name="is_right")
+        nc.gpsimd.dma_start(is_right[:], lab.broadcast_to([P, N]))
+        bias = [held.tile([P, 1], F32, name=f"bias{block}") for block in range(E // P)]
+        for block in range(E // P):
+            nc.gpsimd.dma_start(bias[block][:], b[block * P : (block + 1) * P, :])
+
+        is_wrong = held.tile([P, N], F32, name="is_wrong")
+        nc.vector.tensor_scalar(is_wrong[:], is_right[:], -1.0, 1.0, op0=MULT, op1=ADD)
+
+        tiles = [(piece, block) for piece in range(N // PIECE) for block in range(E // P)]
+        answers = ("right", "wrong")
+
+        def weight_columns(block, answer):
+            first = block * P if answer == "right" else E + block * P
+            return slice(first, first + P)
+
+        u = {}
+        for piece, block in tiles:
+            for answer in answers:
+                u[piece, block, answer] = psum.tile([P, PIECE], F32, name="u_" + answer)
+                nc.tensor.matmul(
+                    u[piece, block, answer][:],
+                    w_skill_sb[:, weight_columns(block, answer)],
+                    skill_sb[:, piece * PIECE : (piece + 1) * PIECE],
+                    start=True,
+                    stop=False,
+                )
+
+        columns = PIECE // PER_COLUMN
+        for piece, block in tiles:
+            looked_up = table_sb[:].indirect(offsets[:, piece * columns : (piece + 1) * columns])
+            for answer in answers:
+                nc.tensor.matmul(
+                    u[piece, block, answer][:],
+                    w_item_sb[:, weight_columns(block, answer)],
+                    looked_up,
+                    start=False,
+                    stop=True,
+                )
+
+        for piece, block in tiles:
+            cols = slice(piece * PIECE, (piece + 1) * PIECE)
+            u_right, u_wrong = u[piece, block, "right"], u[piece, block, "wrong"]
+
+            part_right = work.tile([P, PIECE], F32, name="part_right")
+            nc.vector.tensor_tensor(part_right[:], u_right[:], is_right[:, cols], MULT)
+            part_wrong = work.tile([P, PIECE], F32, name="part_wrong")
+            nc.vector.tensor_tensor(part_wrong[:], u_wrong[:], is_wrong[:, cols], MULT)
+            blend = work.tile([P, PIECE], F32, name="blend")
+            nc.gpsimd.tensor_tensor(blend[:], part_right[:], part_wrong[:], ADD)
+
+            result = work.tile([P, PIECE], F32, name="result")
+            nc.scalar.activation(result[:], blend[:], RELU, bias=bias[block][:])
+            nc.sync.dma_start(out[block * P : (block + 1) * P, cols], result[:])

@@ -21,15 +21,17 @@ def tile_tsakt_kernel(tc, table, skill, w_item, w_skill, b, lab, offs, out):
         tc.tile_pool(name="work", bufs=4) as work,
         tc.psum_pool(name="psum", bufs=4) as psum,
     ):
-        offsets = held.tile([P, N // PER_COLUMN], U16, name="offsets")
-        nc.sync.dma_start(offsets[:], offs)
         w_skill_sb = held.tile([P, 2 * E], BF16, name="w_skill_sb")
-        nc.scalar.dma_start(w_skill_sb[:], w_skill)
         skill_sb = held.tile([P, N], BF16, name="skill_sb")
-        nc.scalar.dma_start(skill_sb[:], skill)
         table_sb = held.tile([P, ITEMS], BF16, name="table_sb")
-        nc.sync.dma_start(table_sb[:], table)
+        offsets = held.tile([P, N // PER_COLUMN], U16, name="offsets")
         w_item_sb = held.tile([P, 2 * E], BF16, name="w_item_sb")
+        nc.sync.dma_start(w_skill_sb[:], w_skill)
+        nc.sync.dma_start(table_sb[:], table)
+        nc.sync.dma_start(offsets[:], offs)
+        for piece in range(N // PIECE):
+            cols = slice(piece * PIECE, (piece + 1) * PIECE)
+            nc.scalar.dma_start(skill_sb[:, cols], skill[:, cols])
         nc.scalar.dma_start(w_item_sb[:], w_item)
 
         is_right = held.tile([P, N], F32, name="is_right")

@@ -10,6 +10,7 @@ N = 1024
 E = 256
 PIECE = 512
 PER_COLUMN = 16
+WARM_UP_MATMULS = 3
 
 FLOPS = 2 * (2 * E) * N * (2 * P)
 
@@ -54,6 +55,14 @@ def tile_tsakt_kernel(tc, table, skill, w_item, w_skill, b, lab, offs, out):
         for piece, block in tiles:
             for answer in answers:
                 u[piece, block, answer] = psum.tile([P, PIECE], F32, name="u_" + answer)
+
+        zeros = held.tile([P, PIECE], BF16, name="zeros")
+        nc.vector.memset(zeros[:], 0.0)
+        for warm in range(WARM_UP_MATMULS):
+            nc.tensor.matmul(u[tiles[0] + (answers[0],)][:], zeros[:, :P], zeros[:], start=True, stop=True)
+
+        for piece, block in tiles:
+            for answer in answers:
                 nc.tensor.matmul(
                     u[piece, block, answer][:],
                     w_skill_sb[:, weight_columns(block, answer)],

@@ -1,7 +1,7 @@
 import concourse.mybir as mybir
 
 BF16, F32, U16 = mybir.dt.bfloat16, mybir.dt.float32, mybir.dt.uint16
-MULT, ADD = mybir.AluOpType.mult, mybir.AluOpType.add
+MULT, ADD, SUBTRACT = mybir.AluOpType.mult, mybir.AluOpType.add, mybir.AluOpType.subtract
 RELU = mybir.ActivationFunctionType.Relu
 
 P = 128
@@ -27,22 +27,23 @@ def tile_tsakt_kernel(tc, table, skill, w_item, w_skill, b, lab, offs, out):
         table_sb = held.tile([P, ITEMS], BF16, name="table_sb")
         offsets = held.tile([P, N // PER_COLUMN], U16, name="offsets")
         w_item_sb = held.tile([P, 2 * E], BF16, name="w_item_sb")
-        nc.sync.dma_start(w_skill_sb[:], w_skill)
-        nc.sync.dma_start(table_sb[:], table)
-        nc.sync.dma_start(offsets[:], offs)
-        for piece in range(N // PIECE):
-            cols = slice(piece * PIECE, (piece + 1) * PIECE)
-            nc.scalar.dma_start(skill_sb[:, cols], skill[:, cols])
-        nc.scalar.dma_start(w_item_sb[:], w_item)
-
         is_right = held.tile([P, N], F32, name="is_right")
-        nc.gpsimd.dma_start(is_right[:], lab.broadcast_to([P, N]))
         bias = [held.tile([P, 1], F32, name=f"bias{block}") for block in range(E // P)]
-        for block in range(E // P):
-            nc.gpsimd.dma_start(bias[block][:], b[block * P : (block + 1) * P, :])
 
-        is_wrong = held.tile([P, N], F32, name="is_wrong")
-        nc.vector.tensor_scalar(is_wrong[:], is_right[:], -1.0, 1.0, op0=MULT, op1=ADD)
+        half = ITEMS // 2
+        quarter = N // 4
+        nc.sync.dma_start(w_skill_sb[:], w_skill)
+        nc.scalar.dma_start(skill_sb[:, :PIECE], skill[:, :PIECE])
+        nc.scalar.dma_start(skill_sb[:, PIECE:], skill[:, PIECE:])
+        nc.sync.dma_start(table_sb[:, :half], table[:, :half])
+        nc.scalar.dma_start(table_sb[:, half:], table[:, half:])
+        nc.sync.dma_start(w_item_sb[:], w_item)
+        nc.sync.dma_start(offsets[:], offs)
+        for part, queue in enumerate((nc.sync, nc.scalar, nc.sync, nc.scalar)):
+            cols = slice(part * quarter, (part + 1) * quarter)
+            queue.dma_start(is_right[:, cols], lab[:, cols].broadcast_to([P, quarter]))
+        for block, queue in enumerate((nc.sync, nc.scalar)):
+            queue.dma_start(bias[block][:], b[block * P : (block + 1) * P, :])
 
         tiles = [(piece, block) for piece in range(N // PIECE) for block in range(E // P)]
         answers = ("right", "wrong")
@@ -89,10 +90,12 @@ def tile_tsakt_kernel(tc, table, skill, w_item, w_skill, b, lab, offs, out):
 
             part_right = work.tile([P, PIECE], F32, name="part_right")
             nc.vector.tensor_tensor(part_right[:], u_right[:], is_right[:, cols], MULT)
-            part_wrong = work.tile([P, PIECE], F32, name="part_wrong")
-            nc.vector.tensor_tensor(part_wrong[:], u_wrong[:], is_wrong[:, cols], MULT)
+            minus_part_wrong = work.tile([P, PIECE], F32, name="minus_part_wrong")
+            nc.vector.scalar_tensor_tensor(
+                minus_part_wrong[:], is_right[:, cols], 1.0, u_wrong[:], op0=SUBTRACT, op1=MULT
+            )
             blend = work.tile([P, PIECE], F32, name="blend")
-            nc.gpsimd.tensor_tensor(blend[:], part_right[:], part_wrong[:], ADD)
+            nc.gpsimd.tensor_tensor(blend[:], part_right[:], minus_part_wrong[:], SUBTRACT)
 
             result = work.tile([P, PIECE], F32, name="result")
             nc.scalar.activation(result[:], blend[:], RELU, bias=bias[block][:])

@@ -1,7 +1,7 @@
 import concourse.mybir as mybir
 
 BF16, F32, U16 = mybir.dt.bfloat16, mybir.dt.float32, mybir.dt.uint16
-MULT, ADD, SUBTRACT = mybir.AluOpType.mult, mybir.AluOpType.add, mybir.AluOpType.subtract
+MULT, ADD, SUBTRACT, MAX = (mybir.AluOpType.mult, mybir.AluOpType.add, mybir.AluOpType.subtract, mybir.AluOpType.max)
 RELU = mybir.ActivationFunctionType.Relu
 
 P = 128
@@ -95,8 +95,11 @@ def tile_tsakt_kernel(tc, table, skill, w_item, w_skill, b, lab, offs, out):
                 minus_part_wrong[:], is_right[:, cols], 1.0, u_wrong[:], op0=SUBTRACT, op1=MULT
             )
             blend = work.tile([P, PIECE], F32, name="blend")
-            nc.gpsimd.tensor_tensor(blend[:], part_right[:], minus_part_wrong[:], SUBTRACT)
-
             result = work.tile([P, PIECE], F32, name="result")
-            nc.scalar.activation(result[:], blend[:], RELU, bias=bias[block][:])
+            if (piece, block) != tiles[-1]:
+                nc.gpsimd.tensor_tensor(blend[:], part_right[:], minus_part_wrong[:], SUBTRACT)
+                nc.scalar.activation(result[:], blend[:], RELU, bias=bias[block][:])
+            else:
+                nc.vector.tensor_tensor(blend[:], part_right[:], minus_part_wrong[:], SUBTRACT)
+                nc.vector.tensor_scalar(result[:], blend[:], bias[block][:], 0.0, op0=ADD, op1=MAX)
             nc.sync.dma_start(out[block * P : (block + 1) * P, cols], result[:])

@@ -1,7 +1,7 @@
 import concourse.mybir as mybir
 
 BF16, F32, U16 = mybir.dt.bfloat16, mybir.dt.float32, mybir.dt.uint16
-MULT, ADD, SUBTRACT, MAX = (mybir.AluOpType.mult, mybir.AluOpType.add, mybir.AluOpType.subtract, mybir.AluOpType.max)
+ADD, MAX = mybir.AluOpType.add, mybir.AluOpType.max
 RELU = mybir.ActivationFunctionType.Relu
 
 P = 128
@@ -10,7 +10,8 @@ N = 1024
 E = 256
 PIECE = 512
 PER_COLUMN = 16
-WARM_UP_MATMULS = 3
+ROWS = 32
+BIG = 2.0 ** 126
 
 FLOPS = 2 * (2 * E) * N * (2 * P)
 
@@ -22,28 +23,32 @@ def tile_tsakt_kernel(tc, table, skill, w_item, w_skill, b, lab, offs, out):
         tc.tile_pool(name="work", bufs=4) as work,
         tc.psum_pool(name="psum", bufs=4) as psum,
     ):
+        pick_rows = held.tile([P, N], F32, name="pick_rows")
+        pick_weights = held.tile([P, 2 * P], BF16, name="pick_weights")
         w_skill_sb = held.tile([P, 2 * E], BF16, name="w_skill_sb")
         skill_sb = held.tile([P, N], BF16, name="skill_sb")
         table_sb = held.tile([P, ITEMS], BF16, name="table_sb")
         offsets = held.tile([P, N // PER_COLUMN], U16, name="offsets")
         w_item_sb = held.tile([P, 2 * E], BF16, name="w_item_sb")
-        is_right = held.tile([P, N], F32, name="is_right")
-        bias = [held.tile([P, 1], F32, name=f"bias{block}") for block in range(E // P)]
+        bias = held.tile([P, E // P], F32, name="bias")
 
         half = ITEMS // 2
-        quarter = N // 4
+        nc.sync.dma_start(pick_rows[:ROWS, :], lab.broadcast_to([ROWS, N]))
+        nc.scalar.dma_start(skill_sb[:], skill)
         nc.sync.dma_start(w_skill_sb[:], w_skill)
-        nc.scalar.dma_start(skill_sb[:, :PIECE], skill[:, :PIECE])
-        nc.scalar.dma_start(skill_sb[:, PIECE:], skill[:, PIECE:])
-        nc.sync.dma_start(table_sb[:, :half], table[:, :half])
-        nc.scalar.dma_start(table_sb[:, half:], table[:, half:])
-        nc.sync.dma_start(w_item_sb[:], w_item)
         nc.sync.dma_start(offsets[:], offs)
-        for part, queue in enumerate((nc.sync, nc.scalar, nc.sync, nc.scalar)):
-            cols = slice(part * quarter, (part + 1) * quarter)
-            queue.dma_start(is_right[:, cols], lab[:, cols].broadcast_to([P, quarter]))
-        for block, queue in enumerate((nc.sync, nc.scalar)):
-            queue.dma_start(bias[block][:], b[block * P : (block + 1) * P, :])
+        nc.sync.dma_start(table_sb[:, :half], table[:, :half])
+        nc.scalar.dma_start(w_item_sb[:], w_item)
+        nc.scalar.dma_start(table_sb[:, half:], table[:, half:])
+        nc.sync.dma_start(bias[:], b.rearrange("(a p) o -> p (a o)", p=P))
+
+        nc.vector.memset(pick_rows[ROWS : 2 * ROWS, :], 1.0)
+        nc.gpsimd.memset(pick_rows[2 * ROWS :, :], 1.0)
+        nc.vector.memset(pick_weights[:], 0.0)
+        nc.vector.memset(pick_weights[:ROWS, :P], BIG / ROWS)
+        nc.vector.memset(pick_weights[ROWS : 2 * ROWS, :P], -BIG / ROWS)
+        nc.vector.memset(pick_weights[:ROWS, P:], -BIG / ROWS)
+        pick_rows_bf16 = pick_rows[:].bitcast(BF16)
 
         tiles = [(piece, block) for piece in range(N // PIECE) for block in range(E // P)]
         answers = ("right", "wrong")
@@ -57,10 +62,15 @@ def tile_tsakt_kernel(tc, table, skill, w_item, w_skill, b, lab, offs, out):
             for answer in answers:
                 u[piece, block, answer] = psum.tile([P, PIECE], F32, name="u_" + answer)
 
-        zeros = held.tile([P, PIECE], BF16, name="zeros")
-        nc.vector.memset(zeros[:], 0.0)
-        for warm in range(WARM_UP_MATMULS):
-            nc.tensor.matmul(u[tiles[0] + (answers[0],)][:], zeros[:, :P], zeros[:], start=True, stop=True)
+        for piece, block in tiles:
+            for number, answer in enumerate(answers):
+                nc.tensor.matmul(
+                    u[piece, block, answer][:],
+                    pick_weights[:, number * P : (number + 1) * P],
+                    pick_rows_bf16[:, 2 * piece * PIECE + 1 : 2 * (piece + 1) * PIECE : 2],
+                    start=True,
+                    stop=False,
+                )
 
         for piece, block in tiles:
             for answer in answers:
@@ -68,7 +78,7 @@ def tile_tsakt_kernel(tc, table, skill, w_item, w_skill, b, lab, offs, out):
                     u[piece, block, answer][:],
                     w_skill_sb[:, weight_columns(block, answer)],
                     skill_sb[:, piece * PIECE : (piece + 1) * PIECE],
-                    start=True,
+                    start=False,
                     stop=False,
                 )
 
@@ -86,20 +96,11 @@ def tile_tsakt_kernel(tc, table, skill, w_item, w_skill, b, lab, offs, out):
 
         for piece, block in tiles:
             cols = slice(piece * PIECE, (piece + 1) * PIECE)
-            u_right, u_wrong = u[piece, block, "right"], u[piece, block, "wrong"]
-
-            part_right = work.tile([P, PIECE], F32, name="part_right")
-            nc.vector.tensor_tensor(part_right[:], u_right[:], is_right[:, cols], MULT)
-            minus_part_wrong = work.tile([P, PIECE], F32, name="minus_part_wrong")
-            nc.vector.scalar_tensor_tensor(
-                minus_part_wrong[:], is_right[:, cols], 1.0, u_wrong[:], op0=SUBTRACT, op1=MULT
-            )
-            blend = work.tile([P, PIECE], F32, name="blend")
+            b_block = bias[:, block : block + 1]
+            from_right = work.tile([P, PIECE], F32, name="from_right")
+            nc.scalar.activation(from_right[:], u[piece, block, "right"][:], RELU, bias=b_block)
             result = work.tile([P, PIECE], F32, name="result")
-            if (piece, block) != tiles[-1]:
-                nc.gpsimd.tensor_tensor(blend[:], part_right[:], minus_part_wrong[:], SUBTRACT)
-                nc.scalar.activation(result[:], blend[:], RELU, bias=bias[block][:])
-            else:
-                nc.vector.tensor_tensor(blend[:], part_right[:], minus_part_wrong[:], SUBTRACT)
-                nc.vector.tensor_scalar(result[:], blend[:], bias[block][:], 0.0, op0=ADD, op1=MAX)
+            nc.vector.scalar_tensor_tensor(
+                result[:], u[piece, block, "wrong"][:], b_block, from_right[:], op0=ADD, op1=MAX
+            )
             nc.sync.dma_start(out[block * P : (block + 1) * P, cols], result[:])

@@ -83,24 +83,29 @@ def tile_tsakt_kernel(tc, table, skill, w_item, w_skill, b, lab, offs, out):
                 )
 
         columns = PIECE // PER_COLUMN
-        for piece, block in tiles:
+        for piece in range(N // PIECE):
             looked_up = table_sb[:].indirect(offsets[:, piece * columns : (piece + 1) * columns])
             for answer in answers:
-                nc.tensor.matmul(
-                    u[piece, block, answer][:],
-                    w_item_sb[:, weight_columns(block, answer)],
-                    looked_up,
-                    start=False,
-                    stop=True,
-                )
+                for block in range(E // P):
+                    nc.tensor.matmul(
+                        u[piece, block, answer][:],
+                        w_item_sb[:, weight_columns(block, answer)],
+                        looked_up,
+                        start=False,
+                        stop=True,
+                    )
 
         for piece, block in tiles:
-            cols = slice(piece * PIECE, (piece + 1) * PIECE)
             b_block = bias[:, block : block + 1]
             from_right = work.tile([P, PIECE], F32, name="from_right")
             nc.scalar.activation(from_right[:], u[piece, block, "right"][:], RELU, bias=b_block)
             result = work.tile([P, PIECE], F32, name="result")
-            nc.vector.scalar_tensor_tensor(
-                result[:], u[piece, block, "wrong"][:], b_block, from_right[:], op0=ADD, op1=MAX
-            )
-            nc.sync.dma_start(out[block * P : (block + 1) * P, cols], result[:])
+            parts = 2 if (piece, block) == tiles[-1] else 1
+            width = PIECE // parts
+            for part in range(parts):
+                sub = slice(part * width, (part + 1) * width)
+                nc.vector.scalar_tensor_tensor(
+                    result[:, sub], u[piece, block, "wrong"][:, sub], b_block, from_right[:, sub], op0=ADD, op1=MAX
+                )
+                first = piece * PIECE + part * width
+                nc.sync.dma_start(out[block * P : (block + 1) * P, first : first + width], result[:, sub])

@@ -1,7 +1,7 @@
 import concourse.mybir as mybir
 
 BF16, F32, U16 = mybir.dt.bfloat16, mybir.dt.float32, mybir.dt.uint16
-ADD, MAX = mybir.AluOpType.add, mybir.AluOpType.max
+MULT, ADD, MAX = mybir.AluOpType.mult, mybir.AluOpType.add, mybir.AluOpType.max
 RELU = mybir.ActivationFunctionType.Relu
 
 P = 128
@@ -20,27 +20,30 @@ def tile_tsakt_kernel(tc, table, skill, w_item, w_skill, b, lab, offs, out):
     nc = tc.nc
     with (
         tc.tile_pool(name="held", bufs=1) as held,
-        tc.tile_pool(name="work", bufs=4) as work,
+        tc.tile_pool(name="work", bufs=2) as work,
         tc.psum_pool(name="psum", bufs=4) as psum,
     ):
-        pick_rows = held.tile([P, N], F32, name="pick_rows")
+        pick_rows = held.tile([P, PIECE], F32, name="pick_rows")
         pick_weights = held.tile([P, 2 * P], BF16, name="pick_weights")
         w_skill_sb = held.tile([P, 2 * E], BF16, name="w_skill_sb")
         skill_sb = held.tile([P, N], BF16, name="skill_sb")
         table_sb = held.tile([P, ITEMS], BF16, name="table_sb")
         offsets = held.tile([P, N // PER_COLUMN], U16, name="offsets")
         w_item_sb = held.tile([P, 2 * E], BF16, name="w_item_sb")
+        is_right = held.tile([P, PIECE], F32, name="is_right")
+        is_wrong = held.tile([P, PIECE], F32, name="is_wrong")
         bias = held.tile([P, E // P], F32, name="bias")
 
         half = ITEMS // 2
-        nc.sync.dma_start(pick_rows[:ROWS, :], lab.broadcast_to([ROWS, N]))
+        nc.sync.dma_start(pick_rows[:ROWS, :], lab[:, PIECE:].broadcast_to([ROWS, PIECE]))
         nc.scalar.dma_start(skill_sb[:], skill)
         nc.sync.dma_start(w_skill_sb[:], w_skill)
         nc.sync.dma_start(offsets[:], offs)
         nc.sync.dma_start(table_sb[:, :half], table[:, :half])
         nc.scalar.dma_start(w_item_sb[:], w_item)
         nc.scalar.dma_start(table_sb[:, half:], table[:, half:])
-        nc.sync.dma_start(bias[:], b.rearrange("(a p) o -> p (a o)", p=P))
+        nc.scalar.dma_start(bias[:], b.rearrange("(a p) o -> p (a o)", p=P))
+        nc.sync.dma_start(is_right[:], lab[:, :PIECE].broadcast_to([P, PIECE]))
 
         nc.vector.memset(pick_rows[ROWS : 2 * ROWS, :], 1.0)
         nc.gpsimd.memset(pick_rows[2 * ROWS :, :], 1.0)
@@ -48,45 +51,49 @@ def tile_tsakt_kernel(tc, table, skill, w_item, w_skill, b, lab, offs, out):
         nc.vector.memset(pick_weights[:ROWS, :P], BIG / ROWS)
         nc.vector.memset(pick_weights[ROWS : 2 * ROWS, :P], -BIG / ROWS)
         nc.vector.memset(pick_weights[:ROWS, P:], -BIG / ROWS)
-        pick_rows_bf16 = pick_rows[:].bitcast(BF16)
+        pick_rows_bf16 = pick_rows[:].bitcast(BF16)[:, 1 : 2 * PIECE : 2]
 
-        tiles = [(piece, block) for piece in range(N // PIECE) for block in range(E // P)]
-        answers = ("right", "wrong")
+        nc.gpsimd.tensor_scalar(is_wrong[:], is_right[:], -1.0, 1.0, op0=MULT, op1=ADD)
+
+        pieces, blocks, answers = range(N // PIECE), range(E // P), ("right", "wrong")
+        picked_piece = pieces[-1]
 
         def weight_columns(block, answer):
             first = block * P if answer == "right" else E + block * P
             return slice(first, first + P)
 
         u = {}
-        for piece, block in tiles:
-            for answer in answers:
-                u[piece, block, answer] = psum.tile([P, PIECE], F32, name="u_" + answer)
+        for piece in pieces:
+            for block in blocks:
+                for answer in answers:
+                    u[piece, block, answer] = psum.tile([P, PIECE], F32, name="u_" + answer)
 
-        for piece, block in tiles:
+        for block in blocks:
             for number, answer in enumerate(answers):
                 nc.tensor.matmul(
-                    u[piece, block, answer][:],
+                    u[picked_piece, block, answer][:],
                     pick_weights[:, number * P : (number + 1) * P],
-                    pick_rows_bf16[:, 2 * piece * PIECE + 1 : 2 * (piece + 1) * PIECE : 2],
+                    pick_rows_bf16,
                     start=True,
                     stop=False,
                 )
 
-        for piece, block in tiles:
-            for answer in answers:
-                nc.tensor.matmul(
-                    u[piece, block, answer][:],
-                    w_skill_sb[:, weight_columns(block, answer)],
-                    skill_sb[:, piece * PIECE : (piece + 1) * PIECE],
-                    start=False,
-                    stop=False,
-                )
+        for piece in pieces:
+            for block in blocks:
+                for answer in answers:
+                    nc.tensor.matmul(
+                        u[piece, block, answer][:],
+                        w_skill_sb[:, weight_columns(block, answer)],
+                        skill_sb[:, piece * PIECE : (piece + 1) * PIECE],
+                        start=(piece != picked_piece),
+                        stop=False,
+                    )
 
         columns = PIECE // PER_COLUMN
-        for piece in range(N // PIECE):
+        for piece in pieces:
             looked_up = table_sb[:].indirect(offsets[:, piece * columns : (piece + 1) * columns])
             for answer in answers:
-                for block in range(E // P):
+                for block in blocks:
                     nc.tensor.matmul(
                         u[piece, block, answer][:],
                         w_item_sb[:, weight_columns(block, answer)],
@@ -95,17 +102,32 @@ def tile_tsakt_kernel(tc, table, skill, w_item, w_skill, b, lab, offs, out):
                         stop=True,
                     )
 
-        for piece, block in tiles:
+        part_right = {}
+        for block in blocks:
+            part_right[block] = work.tile([P, PIECE], F32, name="part_right")
+            nc.vector.scalar_tensor_tensor(
+                part_right[block][:], u[0, block, "right"][:], bias[:, block : block + 1], is_right[:], op0=ADD, op1=MULT
+            )
+        for block in blocks:
+            part_wrong = work.tile([P, PIECE], F32, name="part_wrong")
+            nc.vector.scalar_tensor_tensor(
+                part_wrong[:], u[0, block, "wrong"][:], bias[:, block : block + 1], is_wrong[:], op0=ADD, op1=MULT
+            )
+            result = work.tile([P, PIECE], F32, name="result")
+            nc.vector.tensor_tensor(result[:], part_right[block][:], part_wrong[:], MAX)
+            nc.sync.dma_start(out[block * P : (block + 1) * P, :PIECE], result[:])
+
+        for block in blocks:
             b_block = bias[:, block : block + 1]
             from_right = work.tile([P, PIECE], F32, name="from_right")
-            nc.scalar.activation(from_right[:], u[piece, block, "right"][:], RELU, bias=b_block)
-            result = work.tile([P, PIECE], F32, name="result")
-            parts = 2 if (piece, block) == tiles[-1] else 1
+            nc.scalar.activation(from_right[:], u[picked_piece, block, "right"][:], RELU, bias=b_block)
+            picked = work.tile([P, PIECE], F32, name="picked")
+            parts = 2 if block == blocks[-1] else 1
             width = PIECE // parts
             for part in range(parts):
                 sub = slice(part * width, (part + 1) * width)
                 nc.vector.scalar_tensor_tensor(
-                    result[:, sub], u[piece, block, "wrong"][:, sub], b_block, from_right[:, sub], op0=ADD, op1=MAX
+                    picked[:, sub], u[picked_piece, block, "wrong"][:, sub], b_block, from_right[:, sub], op0=ADD, op1=MAX
                 )
-                first = piece * PIECE + part * width
-                nc.sync.dma_start(out[block * P : (block + 1) * P, first : first + width], result[:, sub])
+                first = picked_piece * PIECE + part * width
+                nc.sync.dma_start(out[block * P : (block + 1) * P, first : first + width], picked[:, sub])

@@ -12,6 +12,7 @@ PIECE = 512
 PER_COLUMN = 16
 ROWS = 32
 BIG = 2.0 ** 126
+WARM_UP_MATMULS = 3
 
 FLOPS = 2 * (2 * E) * N * (2 * P)
 
@@ -45,6 +46,9 @@ def tile_tsakt_kernel(tc, table, skill, w_item, w_skill, b, lab, offs, out):
         nc.scalar.dma_start(bias[:], b.rearrange("(a p) o -> p (a o)", p=P))
         nc.sync.dma_start(is_right[:], lab[:, :PIECE].broadcast_to([P, PIECE]))
 
+        zeros = held.tile([P, PIECE], BF16, name="zeros")
+        nc.gpsimd.memset(zeros[:], 0.0)
+
         nc.vector.memset(pick_rows[ROWS : 2 * ROWS, :], 1.0)
         nc.gpsimd.memset(pick_rows[2 * ROWS :, :], 1.0)
         nc.vector.memset(pick_weights[:], 0.0)
@@ -67,6 +71,9 @@ def tile_tsakt_kernel(tc, table, skill, w_item, w_skill, b, lab, offs, out):
             for block in blocks:
                 for answer in answers:
                     u[piece, block, answer] = psum.tile([P, PIECE], F32, name="u_" + answer)
+
+        for warm in range(WARM_UP_MATMULS):
+            nc.tensor.matmul(u[0, 0, "right"][:], zeros[:, :P], zeros[:], start=True, stop=True)
 
         for block in blocks:
             for number, answer in enumerate(answers):

@@ -12,7 +12,7 @@ PIECE = 512
 PER_COLUMN = 16
 ROWS = 32
 BIG = 2.0 ** 126
-WARM_UP_MATMULS = 3
+WARM_UP_MATMULS = 2
 
 FLOPS = 2 * (2 * E) * N * (2 * P)
 
@@ -47,7 +47,7 @@ def tile_tsakt_kernel(tc, table, skill, w_item, w_skill, b, lab, offs, out):
         nc.sync.dma_start(is_right[:], lab[:, :PIECE].broadcast_to([P, PIECE]))
 
         zeros = held.tile([P, PIECE], BF16, name="zeros")
-        nc.gpsimd.memset(zeros[:], 0.0)
+        nc.vector.memset(zeros[:], 0.0)
 
         nc.vector.memset(pick_rows[ROWS : 2 * ROWS, :], 1.0)
         nc.gpsimd.memset(pick_rows[2 * ROWS :, :], 1.0)
@@ -73,7 +73,7 @@ def tile_tsakt_kernel(tc, table, skill, w_item, w_skill, b, lab, offs, out):
                     u[piece, block, answer] = psum.tile([P, PIECE], F32, name="u_" + answer)
 
         for warm in range(WARM_UP_MATMULS):
-            nc.tensor.matmul(u[0, 0, "right"][:], zeros[:, :P], zeros[:], start=True, stop=True)
+            nc.tensor.matmul(u[picked_piece, 0, "right"][:], zeros[:, :P], zeros[:], start=True, stop=True)
 
         for block in blocks:
             for number, answer in enumerate(answers):

@@ -2,7 +2,7 @@ import concourse.mybir as mybir
 
 BF16, F32, U16 = mybir.dt.bfloat16, mybir.dt.float32, mybir.dt.uint16
 MULT, ADD, MAX = mybir.AluOpType.mult, mybir.AluOpType.add, mybir.AluOpType.max
-RELU = mybir.ActivationFunctionType.Relu
+RELU, IDENTITY = mybir.ActivationFunctionType.Relu, mybir.ActivationFunctionType.Identity
 
 P = 128
 ITEMS = 2048
@@ -57,7 +57,7 @@ def tile_tsakt_kernel(tc, table, skill, w_item, w_skill, b, lab, offs, out):
         nc.vector.memset(pick_weights[:ROWS, P:], -BIG / ROWS)
         pick_rows_bf16 = pick_rows[:].bitcast(BF16)[:, 1 : 2 * PIECE : 2]
 
-        nc.gpsimd.tensor_scalar(is_wrong[:], is_right[:], -1.0, 1.0, op0=MULT, op1=ADD)
+        nc.scalar.activation(is_wrong[:], is_right[:], IDENTITY, bias=1.0, scale=-1.0)
 
         pieces, blocks, answers = range(N // PIECE), range(E // P), ("right", "wrong")
         picked_piece = pieces[-1]

@@ -35,14 +35,12 @@ def tile_tsakt_kernel(tc, table, skill, w_item, w_skill, b, lab, offs, out):
         is_wrong = held.tile([P, PIECE], F32, name="is_wrong")
         bias = held.tile([P, E // P], F32, name="bias")
 
-        half = ITEMS // 2
         nc.sync.dma_start(pick_rows[:ROWS, :], lab[:, PIECE:].broadcast_to([ROWS, PIECE]))
         nc.scalar.dma_start(skill_sb[:], skill)
         nc.sync.dma_start(w_skill_sb[:], w_skill)
         nc.sync.dma_start(offsets[:], offs)
-        nc.sync.dma_start(table_sb[:, :half], table[:, :half])
         nc.scalar.dma_start(w_item_sb[:], w_item)
-        nc.scalar.dma_start(table_sb[:, half:], table[:, half:])
+        nc.sync.dma_start(table_sb[:], table)
         nc.scalar.dma_start(bias[:], b.rearrange("(a p) o -> p (a o)", p=P))
         nc.sync.dma_start(is_right[:], lab[:, :PIECE].broadcast_to([P, PIECE]))
 

@@ -12,7 +12,7 @@ PIECE = 512
 PER_COLUMN = 16
 ROWS = 32
 BIG = 2.0 ** 126
-WARM_UP_MATMULS = 2
+WARM_UP_MATMULS = 12
 
 FLOPS = 2 * (2 * E) * N * (2 * P)
 
@@ -44,7 +44,7 @@ def tile_tsakt_kernel(tc, table, skill, w_item, w_skill, b, lab, offs, out):
         nc.scalar.dma_start(bias[:], b.rearrange("(a p) o -> p (a o)", p=P))
         nc.sync.dma_start(is_right[:], lab[:, :PIECE].broadcast_to([P, PIECE]))
 
-        zeros = held.tile([P, PIECE], BF16, name="zeros")
+        zeros = held.tile([P, P], BF16, name="zeros")
         nc.vector.memset(zeros[:], 0.0)
 
         nc.vector.memset(pick_rows[ROWS : 2 * ROWS, :], 1.0)
@@ -71,7 +71,7 @@ def tile_tsakt_kernel(tc, table, skill, w_item, w_skill, b, lab, offs, out):
                     u[piece, block, answer] = psum.tile([P, PIECE], F32, name="u_" + answer)
 
         for warm in range(WARM_UP_MATMULS):
-            nc.tensor.matmul(u[picked_piece, 0, "right"][:], zeros[:, :P], zeros[:], start=True, stop=True)
+            nc.tensor.matmul(u[picked_piece, 0, "right"][:, :P], zeros[:], zeros[:], start=True, stop=True)
 
         for block in blocks:
             for number, answer in enumerate(answers):

@@ -2,7 +2,7 @@ import concourse.mybir as mybir
 
 BF16, F32, U16 = mybir.dt.bfloat16, mybir.dt.float32, mybir.dt.uint16
 MULT, ADD, MAX = mybir.AluOpType.mult, mybir.AluOpType.add, mybir.AluOpType.max
-RELU, IDENTITY = mybir.ActivationFunctionType.Relu, mybir.ActivationFunctionType.Identity
+RELU = mybir.ActivationFunctionType.Relu
 
 P = 128
 ITEMS = 2048
@@ -10,6 +10,8 @@ N = 1024
 E = 256
 PIECE = 512
 PER_COLUMN = 16
+SQUARE = 32
+RUNS = PIECE // SQUARE
 ROWS = 32
 BIG = 2.0 ** 126
 WARM_UP_MATMULS = 12
@@ -31,18 +33,23 @@ def tile_tsakt_kernel(tc, table, skill, w_item, w_skill, b, lab, offs, out):
         table_sb = held.tile([P, ITEMS], BF16, name="table_sb")
         offsets = held.tile([P, N // PER_COLUMN], U16, name="offsets")
         w_item_sb = held.tile([P, 2 * E], BF16, name="w_item_sb")
-        is_right = held.tile([P, PIECE], F32, name="is_right")
-        is_wrong = held.tile([P, PIECE], F32, name="is_wrong")
+        lab_runs = held.tile([P, SQUARE], F32, name="lab_runs", align_bytes=64)
+        lab_columns = held.tile([P, SQUARE], F32, name="lab_columns", align_bytes=64)
+        spread = held.tile([P, PIECE], BF16, name="spread", align_bytes=64)
+        is_right = held.tile([P, PIECE], BF16, name="is_right", align_bytes=64)
+        is_wrong = held.tile([P, PIECE], BF16, name="is_wrong")
         bias = held.tile([P, E // P], F32, name="bias")
 
         nc.sync.dma_start(pick_rows[:ROWS, :], lab[:, PIECE:].broadcast_to([ROWS, PIECE]))
         nc.scalar.dma_start(skill_sb[:], skill)
         nc.sync.dma_start(w_skill_sb[:], w_skill)
         nc.sync.dma_start(offsets[:], offs)
-        nc.scalar.dma_start(w_item_sb[:], w_item)
         nc.sync.dma_start(table_sb[:], table)
+        runs_of_lab = lab.rearrange("o (run c) -> (o run) c", c=SQUARE)
+        for first in range(0, P, SQUARE):
+            nc.scalar.dma_start(lab_runs[first : first + SQUARE, :], runs_of_lab)
+        nc.scalar.dma_start(w_item_sb[:], w_item)
         nc.scalar.dma_start(bias[:], b.rearrange("(a p) o -> p (a o)", p=P))
-        nc.sync.dma_start(is_right[:], lab[:, :PIECE].broadcast_to([P, PIECE]))
 
         zeros = held.tile([P, P], BF16, name="zeros")
         nc.vector.memset(zeros[:], 0.0)
@@ -55,7 +62,13 @@ def tile_tsakt_kernel(tc, table, skill, w_item, w_skill, b, lab, offs, out):
         nc.vector.memset(pick_weights[:ROWS, P:], -BIG / ROWS)
         pick_rows_bf16 = pick_rows[:].bitcast(BF16)[:, 1 : 2 * PIECE : 2]
 
-        nc.scalar.activation(is_wrong[:], is_right[:], IDENTITY, bias=1.0, scale=-1.0)
+        nc.vector.transpose(lab_columns[:], lab_runs[:])
+        nc.vector.tensor_copy(
+            spread[:].rearrange("p (run c) -> p run c", c=SQUARE),
+            lab_columns[:, :RUNS].unsqueeze(2).to_broadcast([P, RUNS, SQUARE]),
+        )
+        nc.vector.transpose(is_right[:], spread[:])
+        nc.vector.tensor_scalar(is_wrong[:], is_right[:], -1.0, 1.0, op0=MULT, op1=ADD)
 
         pieces, blocks, answers = range(N // PIECE), range(E // P), ("right", "wrong")
         picked_piece = pieces[-1]

@@ -96,16 +96,22 @@ def tile_tsakt_kernel(tc, table, skill, w_item, w_skill, b, lab, offs, out):
                     stop=False,
                 )
 
+        last_tile = (picked_piece, blocks[-1], "wrong")
+
+        def add_skill(piece, block, answer, start, stop):
+            nc.tensor.matmul(
+                u[piece, block, answer][:],
+                w_skill_sb[:, weight_columns(block, answer)],
+                skill_sb[:, piece * PIECE : (piece + 1) * PIECE],
+                start=start,
+                stop=stop,
+            )
+
         for piece in pieces:
             for block in blocks:
                 for answer in answers:
-                    nc.tensor.matmul(
-                        u[piece, block, answer][:],
-                        w_skill_sb[:, weight_columns(block, answer)],
-                        skill_sb[:, piece * PIECE : (piece + 1) * PIECE],
-                        start=(piece != picked_piece),
-                        stop=False,
-                    )
+                    if (piece, block, answer) != last_tile:
+                        add_skill(piece, block, answer, start=(piece != picked_piece), stop=False)
 
         columns = PIECE // PER_COLUMN
         for piece in pieces:
@@ -117,8 +123,9 @@ def tile_tsakt_kernel(tc, table, skill, w_item, w_skill, b, lab, offs, out):
                         w_item_sb[:, weight_columns(block, answer)],
                         looked_up,
                         start=False,
-                        stop=True,
+                        stop=((piece, block, answer) != last_tile),
                     )
+        add_skill(*last_tile, start=False, stop=True)
 
         part_right = {}
         for block in blocks:

@@ -41,13 +41,13 @@ def tile_tsakt_kernel(tc, table, skill, w_item, w_skill, b, lab, offs, out):
         bias = held.tile([P, E // P], F32, name="bias")
 
         nc.sync.dma_start(pick_rows[:ROWS, :], lab[:, PIECE:].broadcast_to([ROWS, PIECE]))
+        runs_of_lab = lab.rearrange("o (run c) -> (o run) c", c=SQUARE)
+        for group, queue in enumerate((nc.scalar, nc.sync, nc.scalar, nc.sync)):
+            queue.dma_start(lab_runs[group * SQUARE : (group + 1) * SQUARE, :], runs_of_lab)
         nc.scalar.dma_start(skill_sb[:], skill)
         nc.sync.dma_start(w_skill_sb[:], w_skill)
-        nc.sync.dma_start(offsets[:], offs)
         nc.sync.dma_start(table_sb[:], table)
-        runs_of_lab = lab.rearrange("o (run c) -> (o run) c", c=SQUARE)
-        for first in range(0, P, SQUARE):
-            nc.scalar.dma_start(lab_runs[first : first + SQUARE, :], runs_of_lab)
+        nc.sync.dma_start(offsets[:], offs)
         nc.scalar.dma_start(w_item_sb[:], w_item)
         nc.scalar.dma_start(bias[:], b.rearrange("(a p) o -> p (a o)", p=P))
 

@@ -9,6 +9,7 @@ ITEMS = 2048
 N = 1024
 E = 256
 PIECE = 512
+HALF = PIECE // 2
 PER_COLUMN = 16
 SQUARE = 32
 RUNS = PIECE // SQUARE
@@ -48,8 +49,8 @@ def tile_tsakt_kernel(tc, table, skill, w_item, w_skill, b, lab, offs, out):
         nc.sync.dma_start(w_skill_sb[:], w_skill)
         nc.sync.dma_start(table_sb[:], table)
         nc.sync.dma_start(offsets[:], offs)
-        nc.scalar.dma_start(w_item_sb[:], w_item)
-        nc.scalar.dma_start(bias[:], b.rearrange("(a p) o -> p (a o)", p=P))
+        nc.sync.dma_start(w_item_sb[:], w_item)
+        nc.sync.dma_start(bias[:], b.rearrange("(a p) o -> p (a o)", p=P))
 
         zeros = held.tile([P, P], BF16, name="zeros")
         nc.vector.memset(zeros[:], 0.0)
@@ -77,55 +78,77 @@ def tile_tsakt_kernel(tc, table, skill, w_item, w_skill, b, lab, offs, out):
             first = block * P if answer == "right" else E + block * P
             return slice(first, first + P)
 
+        last_tile = (picked_piece, blocks[-1], "wrong")
         u = {}
         for piece in pieces:
             for block in blocks:
                 for answer in answers:
-                    u[piece, block, answer] = psum.tile([P, PIECE], F32, name="u_" + answer)
+                    if (piece, block, answer) != last_tile:
+                        u[piece, block, answer] = psum.tile([P, PIECE], F32, name="u_" + answer)
+        last_halves = [
+            psum.tile([P, HALF], F32, name="u_last_0", tag="u_wrong"),
+            psum.tile([P, HALF], F32, name="u_last_1", tag="u_right"),
+        ]
 
         for warm in range(WARM_UP_MATMULS):
             nc.tensor.matmul(u[picked_piece, 0, "right"][:, :P], zeros[:], zeros[:], start=True, stop=True)
 
         for block in blocks:
             for number, answer in enumerate(answers):
-                nc.tensor.matmul(
-                    u[picked_piece, block, answer][:],
-                    pick_weights[:, number * P : (number + 1) * P],
-                    pick_rows_bf16,
-                    start=True,
-                    stop=False,
-                )
-
-        last_tile = (picked_piece, blocks[-1], "wrong")
-
-        def add_skill(piece, block, answer, start, stop):
-            nc.tensor.matmul(
-                u[piece, block, answer][:],
-                w_skill_sb[:, weight_columns(block, answer)],
-                skill_sb[:, piece * PIECE : (piece + 1) * PIECE],
-                start=start,
-                stop=stop,
-            )
+                if (picked_piece, block, answer) != last_tile:
+                    nc.tensor.matmul(
+                        u[picked_piece, block, answer][:],
+                        pick_weights[:, number * P : (number + 1) * P],
+                        pick_rows_bf16,
+                        start=True,
+                        stop=False,
+                    )
 
         for piece in pieces:
             for block in blocks:
                 for answer in answers:
                     if (piece, block, answer) != last_tile:
-                        add_skill(piece, block, answer, start=(piece != picked_piece), stop=False)
+                        nc.tensor.matmul(
+                            u[piece, block, answer][:],
+                            w_skill_sb[:, weight_columns(block, answer)],
+                            skill_sb[:, piece * PIECE : (piece + 1) * PIECE],
+                            start=(piece != picked_piece),
+                            stop=False,
+                        )
 
-        columns = PIECE // PER_COLUMN
+        def looked_up(first, count):
+            return table_sb[:].indirect(offsets[:, first // PER_COLUMN : (first + count) // PER_COLUMN])
+
         for piece in pieces:
-            looked_up = table_sb[:].indirect(offsets[:, piece * columns : (piece + 1) * columns])
             for answer in answers:
                 for block in blocks:
-                    nc.tensor.matmul(
-                        u[piece, block, answer][:],
-                        w_item_sb[:, weight_columns(block, answer)],
-                        looked_up,
-                        start=False,
-                        stop=((piece, block, answer) != last_tile),
-                    )
-        add_skill(*last_tile, start=False, stop=True)
+                    if (piece, block, answer) != last_tile:
+                        nc.tensor.matmul(
+                            u[piece, block, answer][:],
+                            w_item_sb[:, weight_columns(block, answer)],
+                            looked_up(piece * PIECE, PIECE),
+                            start=False,
+                            stop=True,
+                        )
+        last_weights = weight_columns(blocks[-1], "wrong")
+        for half, tile in enumerate(last_halves):
+            nc.tensor.matmul(
+                tile[:],
+                w_item_sb[:, last_weights],
+                looked_up(picked_piece * PIECE + half * HALF, HALF),
+                start=True,
+                stop=False,
+            )
+
+        for half, tile in enumerate(last_halves):
+            first = half * HALF
+            in_skill = picked_piece * PIECE + first
+            nc.tensor.matmul(
+                tile[:], w_skill_sb[:, last_weights], skill_sb[:, in_skill : in_skill + HALF], start=False, stop=False
+            )
+            nc.tensor.matmul(
+                tile[:], pick_weights[:, P:], pick_rows_bf16[:, first : first + HALF], start=False, stop=True
+            )
 
         part_right = {}
         for block in blocks:
@@ -147,12 +170,13 @@ def tile_tsakt_kernel(tc, table, skill, w_item, w_skill, b, lab, offs, out):
             from_right = work.tile([P, PIECE], F32, name="from_right")
             nc.scalar.activation(from_right[:], u[picked_piece, block, "right"][:], RELU, bias=b_block)
             picked = work.tile([P, PIECE], F32, name="picked")
-            parts = 2 if block == blocks[-1] else 1
-            width = PIECE // parts
-            for part in range(parts):
+            if block == blocks[-1]:
+                wrong_parts = last_halves
+            else:
+                wrong_parts = [u[picked_piece, block, "wrong"]]
+            width = PIECE // len(wrong_parts)
+            for part, wrong in enumerate(wrong_parts):
                 sub = slice(part * width, (part + 1) * width)
-                nc.vector.scalar_tensor_tensor(
-                    picked[:, sub], u[picked_piece, block, "wrong"][:, sub], b_block, from_right[:, sub], op0=ADD, op1=MAX
-                )
+                nc.vector.scalar_tensor_tensor(picked[:, sub], wrong[:], b_block, from_right[:, sub], op0=ADD, op1=MAX)
                 first = picked_piece * PIECE + part * width
                 nc.sync.dma_start(out[block * P : (block + 1) * P, first : first + width], picked[:, sub])

@@ -42,11 +42,11 @@ def tile_tsakt_kernel(tc, table, skill, w_item, w_skill, b, lab, offs, out):
         bias = held.tile([P, E // P], F32, name="bias")
 
         nc.sync.dma_start(pick_rows[:ROWS, :], lab[:, PIECE:].broadcast_to([ROWS, PIECE]))
+        nc.scalar.dma_start(skill_sb[:], skill)
+        nc.sync.dma_start(w_skill_sb[:], w_skill)
         runs_of_lab = lab.rearrange("o (run c) -> (o run) c", c=SQUARE)
         for group, queue in enumerate((nc.scalar, nc.sync, nc.scalar, nc.sync)):
             queue.dma_start(lab_runs[group * SQUARE : (group + 1) * SQUARE, :], runs_of_lab)
-        nc.scalar.dma_start(skill_sb[:], skill)
-        nc.sync.dma_start(w_skill_sb[:], w_skill)
         nc.sync.dma_start(table_sb[:], table)
         nc.sync.dma_start(offsets[:], offs)
         nc.sync.dma_start(w_item_sb[:], w_item)

import concourse.mybir as mybir

BF16, F32, U16 = mybir.dt.bfloat16, mybir.dt.float32, mybir.dt.uint16
MULT, ADD, MAX = mybir.AluOpType.mult, mybir.AluOpType.add, mybir.AluOpType.max
RELU = mybir.ActivationFunctionType.Relu

P = 128
ITEMS = 2048
N = 1024
E = 256
PIECE = 512
HALF = PIECE // 2
PER_COLUMN = 16
SQUARE = 32
RUNS = PIECE // SQUARE
ROWS = 32
BIG = 2.0 ** 126
WARM_UP_MATMULS = 12

FLOPS = 2 * (2 * E) * N * (2 * P)


def tile_tsakt_kernel(tc, table, skill, w_item, w_skill, b, lab, offs, out):
    nc = tc.nc
    with (
        tc.tile_pool(name="held", bufs=1) as held,
        tc.tile_pool(name="work", bufs=2) as work,
        tc.psum_pool(name="psum", bufs=4) as psum,
    ):
        pick_rows = held.tile([P, PIECE], F32, name="pick_rows")
        pick_weights = held.tile([P, 2 * P], BF16, name="pick_weights")
        w_skill_sb = held.tile([P, 2 * E], BF16, name="w_skill_sb")
        skill_sb = held.tile([P, N], BF16, name="skill_sb")
        table_sb = held.tile([P, ITEMS], BF16, name="table_sb")
        offsets = held.tile([P, N // PER_COLUMN], U16, name="offsets")
        w_item_sb = held.tile([P, 2 * E], BF16, name="w_item_sb")
        lab_runs = held.tile([P, SQUARE], F32, name="lab_runs", align_bytes=64)
        lab_columns = held.tile([P, SQUARE], F32, name="lab_columns", align_bytes=64)
        spread = held.tile([P, PIECE], BF16, name="spread", align_bytes=64)
        is_right = held.tile([P, PIECE], BF16, name="is_right", align_bytes=64)
        is_wrong = held.tile([P, PIECE], BF16, name="is_wrong")
        bias = held.tile([P, E // P], F32, name="bias")

        nc.sync.dma_start(pick_rows[:ROWS, :], lab[:, PIECE:].broadcast_to([ROWS, PIECE]))
        nc.scalar.dma_start(skill_sb[:], skill)
        nc.sync.dma_start(w_skill_sb[:], w_skill)
        runs_of_lab = lab.rearrange("o (run c) -> (o run) c", c=SQUARE)
        for group, queue in enumerate((nc.scalar, nc.sync, nc.scalar, nc.sync)):
            queue.dma_start(lab_runs[group * SQUARE : (group + 1) * SQUARE, :], runs_of_lab)
        nc.sync.dma_start(table_sb[:], table)
        nc.sync.dma_start(offsets[:], offs)
        nc.sync.dma_start(w_item_sb[:], w_item)
        nc.sync.dma_start(bias[:], b.rearrange("(a p) o -> p (a o)", p=P))

        zeros = held.tile([P, P], BF16, name="zeros")
        nc.vector.memset(zeros[:], 0.0)

        nc.vector.memset(pick_rows[ROWS : 2 * ROWS, :], 1.0)
        nc.gpsimd.memset(pick_rows[2 * ROWS :, :], 1.0)
        nc.vector.memset(pick_weights[:], 0.0)
        nc.vector.memset(pick_weights[:ROWS, :P], BIG / ROWS)
        nc.vector.memset(pick_weights[ROWS : 2 * ROWS, :P], -BIG / ROWS)
        nc.vector.memset(pick_weights[:ROWS, P:], -BIG / ROWS)
        pick_rows_bf16 = pick_rows[:].bitcast(BF16)[:, 1 : 2 * PIECE : 2]

        nc.vector.transpose(lab_columns[:], lab_runs[:])
        nc.vector.tensor_copy(
            spread[:].rearrange("p (run c) -> p run c", c=SQUARE),
            lab_columns[:, :RUNS].unsqueeze(2).to_broadcast([P, RUNS, SQUARE]),
        )
        nc.vector.transpose(is_right[:], spread[:])
        nc.vector.tensor_scalar(is_wrong[:], is_right[:], -1.0, 1.0, op0=MULT, op1=ADD)

        pieces, blocks, answers = range(N // PIECE), range(E // P), ("right", "wrong")
        picked_piece = pieces[-1]

        def weight_columns(block, answer):
            first = block * P if answer == "right" else E + block * P
            return slice(first, first + P)

        last_tile = (picked_piece, blocks[-1], "wrong")
        u = {}
        for piece in pieces:
            for block in blocks:
                for answer in answers:
                    if (piece, block, answer) != last_tile:
                        u[piece, block, answer] = psum.tile([P, PIECE], F32, name="u_" + answer)
        last_halves = [
            psum.tile([P, HALF], F32, name="u_last_0", tag="u_wrong"),
            psum.tile([P, HALF], F32, name="u_last_1", tag="u_right"),
        ]

        for warm in range(WARM_UP_MATMULS):
            nc.tensor.matmul(u[picked_piece, 0, "right"][:, :P], zeros[:], zeros[:], start=True, stop=True)

        for block in blocks:
            for number, answer in enumerate(answers):
                if (picked_piece, block, answer) != last_tile:
                    nc.tensor.matmul(
                        u[picked_piece, block, answer][:],
                        pick_weights[:, number * P : (number + 1) * P],
                        pick_rows_bf16,
                        start=True,
                        stop=False,
                    )

        for piece in pieces:
            for block in blocks:
                for answer in answers:
                    if (piece, block, answer) != last_tile:
                        nc.tensor.matmul(
                            u[piece, block, answer][:],
                            w_skill_sb[:, weight_columns(block, answer)],
                            skill_sb[:, piece * PIECE : (piece + 1) * PIECE],
                            start=(piece != picked_piece),
                            stop=False,
                        )

        def looked_up(first, count):
            return table_sb[:].indirect(offsets[:, first // PER_COLUMN : (first + count) // PER_COLUMN])

        for piece in pieces:
            for answer in answers:
                for block in blocks:
                    if (piece, block, answer) != last_tile:
                        nc.tensor.matmul(
                            u[piece, block, answer][:],
                            w_item_sb[:, weight_columns(block, answer)],
                            looked_up(piece * PIECE, PIECE),
                            start=False,
                            stop=True,
                        )
        last_weights = weight_columns(blocks[-1], "wrong")
        for half, tile in enumerate(last_halves):
            nc.tensor.matmul(
                tile[:],
                w_item_sb[:, last_weights],
                looked_up(picked_piece * PIECE + half * HALF, HALF),
                start=True,
                stop=False,
            )

        for half, tile in enumerate(last_halves):
            first = half * HALF
            in_skill = picked_piece * PIECE + first
            nc.tensor.matmul(
                tile[:], w_skill_sb[:, last_weights], skill_sb[:, in_skill : in_skill + HALF], start=False, stop=False
            )
            nc.tensor.matmul(
                tile[:], pick_weights[:, P:], pick_rows_bf16[:, first : first + HALF], start=False, stop=True
            )

        part_right = {}
        for block in blocks:
            part_right[block] = work.tile([P, PIECE], F32, name="part_right")
            nc.vector.scalar_tensor_tensor(
                part_right[block][:], u[0, block, "right"][:], bias[:, block : block + 1], is_right[:], op0=ADD, op1=MULT
            )
        for block in blocks:
            part_wrong = work.tile([P, PIECE], F32, name="part_wrong")
            nc.vector.scalar_tensor_tensor(
                part_wrong[:], u[0, block, "wrong"][:], bias[:, block : block + 1], is_wrong[:], op0=ADD, op1=MULT
            )
            result = work.tile([P, PIECE], F32, name="result")
            nc.vector.tensor_tensor(result[:], part_right[block][:], part_wrong[:], MAX)
            nc.sync.dma_start(out[block * P : (block + 1) * P, :PIECE], result[:])

        for block in blocks:
            b_block = bias[:, block : block + 1]
            from_right = work.tile([P, PIECE], F32, name="from_right")
            nc.scalar.activation(from_right[:], u[picked_piece, block, "right"][:], RELU, bias=b_block)
            picked = work.tile([P, PIECE], F32, name="picked")
            if block == blocks[-1]:
                wrong_parts = last_halves
            else:
                wrong_parts = [u[picked_piece, block, "wrong"]]
            width = PIECE // len(wrong_parts)
            for part, wrong in enumerate(wrong_parts):
                sub = slice(part * width, (part + 1) * width)
                nc.vector.scalar_tensor_tensor(picked[:, sub], wrong[:], b_block, from_right[:, sub], op0=ADD, op1=MAX)
                first = picked_piece * PIECE + part * width
                nc.sync.dma_start(out[block * P : (block + 1) * P, first : first + width], picked[:, sub])
